import numpy as np
import ml_dtypes


def mxq(x, axis, fmt="e4m3"):
    dtype, down = {"e4m3": (ml_dtypes.float8_e4m3fn, 7), "e5m2": (ml_dtypes.float8_e5m2, 14)}[fmt]
    v = np.moveaxis(np.asarray(x, np.float32).astype(ml_dtypes.bfloat16).astype(np.float64), axis, -1)
    blocks = v.reshape(v.shape[:-1] + (-1, 32))
    amax = np.abs(blocks).max(-1, keepdims=True)
    byte = np.maximum(np.where(amax > 0, np.frexp(amax)[1] - 1 + 127, 0) - down, 1)
    scale = np.exp2(byte - 127.0)
    codes = (blocks / scale).astype(np.float32).astype(dtype).astype(np.float64)
    return np.moveaxis((codes * scale).reshape(v.shape), -1, axis)


WIDE = False


def mx_kscale(k):
    if not WIDE:
        return np.ones(k)
    levels = np.array([10, -10, 5, -5, 0])
    a = np.random.permutation(np.resize(levels, k // 512 * 4)).reshape(k // 512, 4)
    idx = np.arange(k)
    return np.exp2(a[idx // 512, idx % 128 // 32])


BF16 = ml_dtypes.bfloat16


def bf(x):
    return np.asarray(x, np.float32).astype(BF16)


def f64(x):
    return np.asarray(x).astype(np.float64)


B, C, H, W, F, KH, KW = 8, 512, 18, 16, 128, 3, 3
K = KH * KW * C
SPARSITY = 0.7


def extract_patches(x, kh, kw):
    bb, s1, s2, cc = x.shape
    o1, o2 = s1 - kh + 1, s2 - kw + 1
    pats = np.stack([x[:, i:i + o1, j:j + o2, :] for i in range(kh) for j in range(kw)], axis=3)
    return pats.reshape(bb, o1, o2, kh * kw * cc)


def setup_inputs():
    s = mx_kscale(C)
    limit = np.sqrt(6.0 / (F + K))
    vals = np.random.uniform(-limit, limit, (F, K))
    mask = np.random.random((F, K)) >= SPARSITY
    mask[:, ::32] = True
    return {"inputs": bf(np.random.standard_normal((B, C, H, W)) * s[None, :, None, None]),
            "kernel": bf(vals * mask / np.tile(s, KH * KW)[None, :])}


def reference(inputs, kernel):
    x = np.transpose(f64(inputs), (0, 3, 2, 1))
    p = extract_patches(x, KH, KW)
    p2 = np.ascontiguousarray(p.reshape(-1, K))
    wt = np.ascontiguousarray(f64(kernel).T)
    out = mxq(p2, 1, "e4m3") @ mxq(wt, 0, "e4m3")
    return out.reshape(p.shape[:3] + (F,)).transpose(0, 3, 1, 2)

@@ -1,0 +1,118 @@
+import concourse.mybir as mybir
+from concourse.masks import make_identity
+
+F32 = mybir.dt.float32
+BF16 = mybir.dt.bfloat16
+U32 = mybir.dt.uint32
+U8 = mybir.dt.uint8
+FP8X4 = mybir.dt.float8_e4m3fn_x4
+ADD = mybir.AluOpType.add
+
+P = 128
+B, C, H, W, F = 8, 512, 18, 16, 128
+KH, KW = 3, 3
+OA, OD = W - KH + 1, H - KW + 1
+GB = 4
+NG = B // GB
+ROW = GB * W
+DT = 8
+NPASS = KH * KW
+
+FLOPS = 2 * B * OA * OD * KH * KW * C * F
+
+
+def tile_sparseconv2d_kernel(tc, inputs, kernel, out):
+    nc = tc.nc
+    with tc.tile_pool(name="keep", bufs=1) as keep, tc.psum_pool(name="psum", bufs=8) as psum:
+        ident = keep.tile([P, P], F32, name="ident")
+        make_identity(nc, ident[:])
+
+        kw = keep.tile([P, NPASS * C], BF16, name="kw")
+        for i in range(KH):
+            cols = slice(i * KW * C, (i + 1) * KW * C)
+            nc.sync.dma_start(out=kw[:, cols], in_=kernel[:, cols])
+        raws = []
+        for g in range(NG):
+            raw = keep.tile([P, GB, 4, H * W], BF16, name="raw%d" % g)
+            raws.append(raw)
+            for b in range(GB):
+                nc.sync.dma_start(
+                    out=raw[:, b, :, :],
+                    in_=inputs[g * GB + b].rearrange("(p t) h w -> p t (h w)", t=4),
+                )
+
+        kwords = kw[:].bitcast(F32).rearrange("p (g q u) -> p g u q", q=P, u=2)
+        wgrp = keep.tile([P, NPASS * 4 * F], BF16, name="wgrp", align_bytes=64)
+        wgrp_words = wgrp[:].bitcast(F32).rearrange("p (g f u) -> p g f u", f=F, u=2)
+        wcodes = keep.tile([P, NPASS * F], U32, name="wcodes", align_bytes=64)
+        wscales = keep.tile([P, NPASS * F], U8, name="wscales", align_bytes=64)
+        for g0 in range(0, NPASS, 2):
+            n = min(2, NPASS - g0)
+            wt = psum.tile([P, 2, 2, F], F32, name="wt", tag="bank")
+            for k in range(n):
+                for u in range(2):
+                    nc.tensor.transpose(wt[:, k, u, :], kwords[:, g0 + k, u, :], ident[:])
+            src = wt[:, 0:n, :, :].rearrange("p g u f -> p g f u")
+            dst = wgrp_words[:, g0:g0 + n, :, :]
+            if (g0 // 2) % 2 == 0:
+                nc.scalar.copy(out=dst, in_=src)
+            else:
+                nc.vector.tensor_copy(out=dst, in_=src)
+        for g0 in range(0, NPASS, 2):
+            n = min(2, NPASS - g0)
+            nc.vector.quantize_mx(
+                out=wcodes[:, g0 * F:(g0 + n) * F].bitcast(FP8X4),
+                scales=wscales[:, g0 * F:(g0 + n) * F],
+                in_=wgrp[:, g0 * 4 * F:(g0 + n) * 4 * F],
+            )
+
+        for g in range(NG):
+            raw = raws[g]
+            grp = keep.tile([P, H * ROW * 4], BF16, name="grp%d" % g, align_bytes=64)
+            grp5 = grp[:].rearrange("p (h b w t) -> p h b w t", h=H, b=GB, w=W)
+            xcodes = keep.tile([P, H * ROW], U32, name="xcodes%d" % g, align_bytes=64)
+            xscales = keep.tile([P, H * ROW], U8, name="xscales%d" % g, align_bytes=64)
+            for b in range(GB):
+                if b == 1:
+                    nc.scalar.copy(
+                        out=grp5[:, :, b, :, :],
+                        in_=raw[:, b, :, :].rearrange("p t (h w) -> p h w t", w=W),
+                    )
+                else:
+                    nc.vector.tensor_copy(
+                        out=grp5[:, :, b, :, :].rearrange("p h (q i) t -> p h q t i", i=4),
+                        in_=raw[:, b, :, :].rearrange("p t (h q i) -> p h q t i", q=4, i=4),
+                    )
+            for h0, h1 in ((0, 8), (8, 10), (10, 18)):
+                nc.vector.quantize_mx(
+                    out=xcodes[:, h0 * ROW:h1 * ROW].bitcast(FP8X4),
+                    scales=xscales[:, h0 * ROW:h1 * ROW],
+                    in_=grp[:, h0 * ROW * 4:h1 * ROW * 4],
+                )
+            osb = keep.tile([P, GB * OA * OD], F32, name="osb%d" % g)
+            osb4 = osb[:].rearrange("p (b a d) -> p b a d", b=GB, a=OA)
+            for i in range(KH):
+                for dt in range(OD // DT):
+                    y = psum.tile([P, DT * ROW], F32, name="y", tag="bank")
+                    for j in range(KW):
+                        k = i * KW + j
+                        c0 = (dt * DT + j) * ROW
+                        nc.tensor.matmul_mx(
+                            out=y[:],
+                            lhsT=wcodes[:, k * F:(k + 1) * F].bitcast(FP8X4),
+                            lhsT_scale=wscales[:, k * F:(k + 1) * F],
+                            rhs=xcodes[:, c0:c0 + DT * ROW].bitcast(FP8X4),
+                            rhs_scale=xscales[:, c0:c0 + DT * ROW],
+                            start=(j == 0),
+                            stop=(j == KW - 1),
+                        )
+                    src = y[:].rearrange("p (d b w) -> p b w d", d=DT, b=GB)[:, :, i:i + OA, :]
+                    dst = osb4[:, :, :, dt * DT:(dt + 1) * DT]
+                    if i == 0:
+                        nc.scalar.copy(out=dst, in_=src)
+                    else:
+                        nc.vector.tensor_tensor(out=dst, in0=src, in1=dst, op=ADD)
+            nc.sync.dma_start(
+                out=out[g * GB:(g + 1) * GB].rearrange("b f a d -> f b (a d)"),
+                in_=osb[:].rearrange("p (b s) -> p b s", b=GB),
+            )

@@ -3,6 +3,7 @@ from concourse.masks import make_identity
 
 F32 = mybir.dt.float32
 BF16 = mybir.dt.bfloat16
+I32 = mybir.dt.int32
 U32 = mybir.dt.uint32
 U8 = mybir.dt.uint8
 FP8X4 = mybir.dt.float8_e4m3fn_x4
@@ -12,53 +13,78 @@ P = 128
 B, C, H, W, F = 8, 512, 18, 16, 128
 KH, KW = 3, 3
 OA, OD = W - KH + 1, H - KW + 1
-GB = 4
+GB = 2
 NG = B // GB
 ROW = GB * W
-DT = 8
+N = OD * ROW
 NPASS = KH * KW
+SPLIT = 12
 
 FLOPS = 2 * B * OA * OD * KH * KW * C * F
 
 
 def tile_sparseconv2d_kernel(tc, inputs, kernel, out):
     nc = tc.nc
-    with tc.tile_pool(name="keep", bufs=1) as keep, tc.psum_pool(name="psum", bufs=8) as psum:
+    with tc.tile_pool(name="keep", bufs=1) as keep, tc.psum_pool(name="psum", bufs=8) as psum, tc.manual_schedule():
         ident = keep.tile([P, P], F32, name="ident")
         make_identity(nc, ident[:])
+        xscales = keep.tile([P, NG, H * ROW], U8, name="xscales", align_bytes=64)
+        nc.vector.memset(xscales[:].rearrange("p g c -> p (g c)").bitcast(I32), 0)
 
         kw = keep.tile([P, NPASS * C], BF16, name="kw")
-        for i in range(KH):
-            cols = slice(i * KW * C, (i + 1) * KW * C)
+        raw = keep.tile([P, B, 4, H * W], BF16, name="raw")
+
+        def load_image(b):
+            nc.sync.dma_start(out=raw[:, b, :, :], in_=inputs[b].rearrange("(p t) h w -> p t (h w)", t=4))
+
+        load_image(0)
+        load_image(1)
+        for g0 in range(0, NPASS, 2):
+            cols = slice(g0 * C, min(g0 + 2, NPASS) * C)
             nc.sync.dma_start(out=kw[:, cols], in_=kernel[:, cols])
-        raws = []
-        for g in range(NG):
-            raw = keep.tile([P, GB, 4, H * W], BF16, name="raw%d" % g)
-            raws.append(raw)
-            for b in range(GB):
-                nc.sync.dma_start(
-                    out=raw[:, b, :, :],
-                    in_=inputs[g * GB + b].rearrange("(p t) h w -> p t (h w)", t=4),
-                )
+        for b in range(2, B):
+            load_image(b)
 
         kwords = kw[:].bitcast(F32).rearrange("p (g q u) -> p g u q", q=P, u=2)
         wgrp = keep.tile([P, NPASS * 4 * F], BF16, name="wgrp", align_bytes=64)
         wgrp_words = wgrp[:].bitcast(F32).rearrange("p (g f u) -> p g f u", f=F, u=2)
         wcodes = keep.tile([P, NPASS * F], U32, name="wcodes", align_bytes=64)
         wscales = keep.tile([P, NPASS * F], U8, name="wscales", align_bytes=64)
-        for g0 in range(0, NPASS, 2):
+        grp = keep.tile([P, NG, H * ROW * 4], BF16, name="grp", align_bytes=64)
+        xcodes = keep.tile([P, NG, H * ROW], U32, name="xcodes", align_bytes=64)
+        xshift = keep.tile([P, NG, N], U8, name="xshift", align_bytes=64)
+        osb = keep.tile([P, NG, GB * OA * OD], F32, name="osb")
+        banks = {}
+
+        def regroup(b, engine, h0, h1):
+            dst = grp[:, b // GB, :].rearrange("p (h b w t) -> p h b w t", h=H, b=GB, w=W)[:, h0:h1, b % GB, :, :]
+            src = raw[:, b, :, h0 * W:h1 * W]
+            if engine == "v":
+                nc.vector.tensor_copy(
+                    out=dst.rearrange("p h (q i) t -> p h q t i", i=4),
+                    in_=src.rearrange("p t (h q i) -> p h q t i", q=4, i=4),
+                )
+            else:
+                nc.scalar.copy(out=dst, in_=src.rearrange("p t (h w) -> p h w t", w=W))
+
+        def quantise_image(g):
+            for h0, h1 in ((0, OD), (OD, H)):
+                nc.vector.quantize_mx(
+                    out=xcodes[:, g, h0 * ROW:h1 * ROW].bitcast(FP8X4),
+                    scales=xscales[:, g, h0 * ROW:h1 * ROW],
+                    in_=grp[:, g, h0 * ROW * 4:h1 * ROW * 4],
+                )
+            nc.vector.tensor_copy(out=xshift[:, g, :].bitcast(I32), in_=xscales[:, g, ROW:ROW + N].bitcast(I32))
+
+        def weights_transpose(g0):
             n = min(2, NPASS - g0)
             wt = psum.tile([P, 2, 2, F], F32, name="wt", tag="bank")
             for k in range(n):
                 for u in range(2):
                     nc.tensor.transpose(wt[:, k, u, :], kwords[:, g0 + k, u, :], ident[:])
-            src = wt[:, 0:n, :, :].rearrange("p g u f -> p g f u")
-            dst = wgrp_words[:, g0:g0 + n, :, :]
-            if (g0 // 2) % 2 == 0:
-                nc.scalar.copy(out=dst, in_=src)
-            else:
-                nc.vector.tensor_copy(out=dst, in_=src)
-        for g0 in range(0, NPASS, 2):
+            nc.scalar.copy(out=wgrp_words[:, g0:g0 + n, :, :], in_=wt[:, 0:n, :, :].rearrange("p g u f -> p g f u"))
+
+        def weights_quantise(g0):
             n = min(2, NPASS - g0)
             nc.vector.quantize_mx(
                 out=wcodes[:, g0 * F:(g0 + n) * F].bitcast(FP8X4),
@@ -66,53 +92,79 @@ def tile_sparseconv2d_kernel(tc, inputs, kernel, out):
                 in_=wgrp[:, g0 * 4 * F:(g0 + n) * 4 * F],
             )
 
-        for g in range(NG):
-            raw = raws[g]
-            grp = keep.tile([P, H * ROW * 4], BF16, name="grp%d" % g, align_bytes=64)
-            grp5 = grp[:].rearrange("p (h b w t) -> p h b w t", h=H, b=GB, w=W)
-            xcodes = keep.tile([P, H * ROW], U32, name="xcodes%d" % g, align_bytes=64)
-            xscales = keep.tile([P, H * ROW], U8, name="xscales%d" % g, align_bytes=64)
-            for b in range(GB):
-                if b == 1:
-                    nc.scalar.copy(
-                        out=grp5[:, :, b, :, :],
-                        in_=raw[:, b, :, :].rearrange("p t (h w) -> p h w t", w=W),
-                    )
-                else:
-                    nc.vector.tensor_copy(
-                        out=grp5[:, :, b, :, :].rearrange("p h (q i) t -> p h q t i", i=4),
-                        in_=raw[:, b, :, :].rearrange("p t (h q i) -> p h q t i", q=4, i=4),
-                    )
-            for h0, h1 in ((0, 8), (8, 10), (10, 18)):
-                nc.vector.quantize_mx(
-                    out=xcodes[:, h0 * ROW:h1 * ROW].bitcast(FP8X4),
-                    scales=xscales[:, h0 * ROW:h1 * ROW],
-                    in_=grp[:, h0 * ROW * 4:h1 * ROW * 4],
+        def multiply(g, i):
+            y = psum.tile([P, N], F32, name="y", tag="bank")
+            banks[(g, i)] = y
+            for j in range(KW):
+                k = i * KW + j
+                plane = xshift[:, g, :] if j == 1 else xscales[:, g, j * ROW:j * ROW + N]
+                nc.tensor.matmul_mx(
+                    out=y[:],
+                    lhsT=wcodes[:, k * F:(k + 1) * F].bitcast(FP8X4),
+                    lhsT_scale=wscales[:, k * F:(k + 1) * F],
+                    rhs=xcodes[:, g, j * ROW:j * ROW + N].bitcast(FP8X4),
+                    rhs_scale=plane,
+                    start=(j == 0),
+                    stop=(j == KW - 1),
                 )
-            osb = keep.tile([P, GB * OA * OD], F32, name="osb%d" % g)
-            osb4 = osb[:].rearrange("p (b a d) -> p b a d", b=GB, a=OA)
-            for i in range(KH):
-                for dt in range(OD // DT):
-                    y = psum.tile([P, DT * ROW], F32, name="y", tag="bank")
-                    for j in range(KW):
-                        k = i * KW + j
-                        c0 = (dt * DT + j) * ROW
-                        nc.tensor.matmul_mx(
-                            out=y[:],
-                            lhsT=wcodes[:, k * F:(k + 1) * F].bitcast(FP8X4),
-                            lhsT_scale=wscales[:, k * F:(k + 1) * F],
-                            rhs=xcodes[:, c0:c0 + DT * ROW].bitcast(FP8X4),
-                            rhs_scale=xscales[:, c0:c0 + DT * ROW],
-                            start=(j == 0),
-                            stop=(j == KW - 1),
-                        )
-                    src = y[:].rearrange("p (d b w) -> p b w d", d=DT, b=GB)[:, :, i:i + OA, :]
-                    dst = osb4[:, :, :, dt * DT:(dt + 1) * DT]
-                    if i == 0:
-                        nc.scalar.copy(out=dst, in_=src)
-                    else:
-                        nc.vector.tensor_tensor(out=dst, in0=src, in1=dst, op=ADD)
+
+        def collect(g, i):
+            src = banks[(g, i)][:].rearrange("p (d b w) -> p b w d", d=OD, b=GB)[:, :, i:i + OA, :]
+            dst = osb[:, g, :].rearrange("p (b a d) -> p b a d", b=GB, a=OA)
+            if i == 0:
+                nc.scalar.copy(out=dst, in_=src)
+            else:
+                nc.vector.tensor_tensor(out=dst, in0=src, in1=dst, op=ADD)
+
+        def store(g):
             nc.sync.dma_start(
                 out=out[g * GB:(g + 1) * GB].rearrange("b f a d -> f b (a d)"),
-                in_=osb[:].rearrange("p (b s) -> p b s", b=GB),
+                in_=osb[:, g, :].rearrange("p (b s) -> p b s", b=GB),
             )
+
+        regroup(0, "v", 0, H)
+        regroup(1, "v", 0, SPLIT)
+        regroup(1, "s", SPLIT, H)
+        quantise_image(0)
+        for g0 in (0, 2, 4):
+            weights_transpose(g0)
+            weights_quantise(g0)
+        weights_transpose(6)
+        regroup(2, "v", 0, H)
+        weights_quantise(6)
+        weights_transpose(8)
+        weights_quantise(8)
+        regroup(3, "s", SPLIT, H)
+        regroup(3, "v", 0, SPLIT)
+        for i in range(KH):
+            multiply(0, i)
+        collect(0, 0)
+        quantise_image(1)
+        regroup(4, "s", 0, H)
+        regroup(5, "v", 0, H)
+        for i in range(KH):
+            multiply(1, i)
+        regroup(6, "s", 0, H)
+        quantise_image(2)
+        collect(0, 1)
+        collect(0, 2)
+        store(0)
+        collect(1, 0)
+        regroup(7, "v", 0, SPLIT)
+        regroup(7, "s", SPLIT, H)
+        quantise_image(3)
+        for i in range(KH):
+            multiply(2, i)
+        collect(2, 0)
+        collect(1, 1)
+        collect(1, 2)
+        store(1)
+        collect(2, 1)
+        collect(2, 2)
+        store(2)
+        for i in range(KH):
+            multiply(3, i)
+        collect(3, 0)
+        collect(3, 1)
+        collect(3, 2)
+        store(3)

@@ -18,7 +18,6 @@ NG = B // GB
 ROW = GB * W
 N = OD * ROW
 NPASS = KH * KW
-SPLIT = 12
 
 FLOPS = 2 * B * OA * OD * KH * KW * C * F
 
@@ -37,11 +36,14 @@ def tile_sparseconv2d_kernel(tc, inputs, kernel, out):
         def load_image(b):
             nc.sync.dma_start(out=raw[:, b, :, :], in_=inputs[b].rearrange("(p t) h w -> p t (h w)", t=4))
 
+        def load_weights(g0):
+            cols = slice(g0 * C, min(g0 + 2, NPASS) * C)
+            nc.sync.dma_start(out=kw[:, cols], in_=kernel[:, cols])
+
         load_image(0)
         load_image(1)
         for g0 in range(0, NPASS, 2):
-            cols = slice(g0 * C, min(g0 + 2, NPASS) * C)
-            nc.sync.dma_start(out=kw[:, cols], in_=kernel[:, cols])
+            load_weights(g0)
         for b in range(2, B):
             load_image(b)
 
@@ -76,13 +78,16 @@ def tile_sparseconv2d_kernel(tc, inputs, kernel, out):
                 )
             nc.vector.tensor_copy(out=xshift[:, g, :].bitcast(I32), in_=xscales[:, g, ROW:ROW + N].bitcast(I32))
 
-        def weights_transpose(g0):
+        def weights_transpose(g0, engine="s"):
             n = min(2, NPASS - g0)
             wt = psum.tile([P, 2, 2, F], F32, name="wt", tag="bank")
             for k in range(n):
                 for u in range(2):
                     nc.tensor.transpose(wt[:, k, u, :], kwords[:, g0 + k, u, :], ident[:])
-            nc.scalar.copy(out=wgrp_words[:, g0:g0 + n, :, :], in_=wt[:, 0:n, :, :].rearrange("p g u f -> p g f u"))
+            if engine == "s":
+                nc.scalar.copy(out=wgrp_words[:, g0:g0 + n, :, :], in_=wt[:, 0:n, :, :].rearrange("p g u f -> p g f u"))
+            else:
+                nc.vector.tensor_copy(out=wgrp_words[:, g0:g0 + n, :, :], in_=wt[:, 0:n, :, :].rearrange("p g u f -> p g f u"))
 
         def weights_quantise(g0):
             n = min(2, NPASS - g0)
@@ -92,25 +97,45 @@ def tile_sparseconv2d_kernel(tc, inputs, kernel, out):
                 in_=wgrp[:, g0 * 4 * F:(g0 + n) * 4 * F],
             )
 
-        def multiply(g, i):
-            y = psum.tile([P, N], F32, name="y", tag="bank")
-            banks[(g, i)] = y
+        def multiply(g, i, d0=0, d1=OD):
+            n = (d1 - d0) * ROW
+            y = psum.tile([P, n], F32, name="y", tag="bank")
+            banks[(g, i, d0)] = y
             for j in range(KW):
                 k = i * KW + j
-                plane = xshift[:, g, :] if j == 1 else xscales[:, g, j * ROW:j * ROW + N]
+                c0 = (d0 + j) * ROW
+                plane = xshift[:, g, c0 - ROW:c0 - ROW + n] if j == 1 else xscales[:, g, c0:c0 + n]
                 nc.tensor.matmul_mx(
                     out=y[:],
                     lhsT=wcodes[:, k * F:(k + 1) * F].bitcast(FP8X4),
                     lhsT_scale=wscales[:, k * F:(k + 1) * F],
-                    rhs=xcodes[:, g, j * ROW:j * ROW + N].bitcast(FP8X4),
+                    rhs=xcodes[:, g, c0:c0 + n].bitcast(FP8X4),
                     rhs_scale=plane,
                     start=(j == 0),
                     stop=(j == KW - 1),
                 )
 
-        def collect(g, i):
-            src = banks[(g, i)][:].rearrange("p (d b w) -> p b w d", d=OD, b=GB)[:, :, i:i + OA, :]
-            dst = osb[:, g, :].rearrange("p (b a d) -> p b a d", b=GB, a=OA)
+        def multiply_shift_major(g):
+            ys = [psum.tile([P, N], F32, name="y%d" % i, tag="bank") for i in range(KH)]
+            for j in range(KW):
+                for i in range(KH):
+                    banks[(g, i, 0)] = ys[i]
+                    k = i * KW + j
+                    c0 = j * ROW
+                    plane = xshift[:, g, :] if j == 1 else xscales[:, g, c0:c0 + N]
+                    nc.tensor.matmul_mx(
+                        out=ys[i][:],
+                        lhsT=wcodes[:, k * F:(k + 1) * F].bitcast(FP8X4),
+                        lhsT_scale=wscales[:, k * F:(k + 1) * F],
+                        rhs=xcodes[:, g, c0:c0 + N].bitcast(FP8X4),
+                        rhs_scale=plane,
+                        start=(j == 0),
+                        stop=(j == KW - 1),
+                    )
+
+        def collect(g, i, d0=0, d1=OD):
+            src = banks[(g, i, d0)][:].rearrange("p (d b w) -> p b w d", d=d1 - d0, b=GB)[:, :, i:i + OA, :]
+            dst = osb[:, g, :].rearrange("p (b a d) -> p b a d", b=GB, a=OA)[:, :, :, d0:d1]
             if i == 0:
                 nc.scalar.copy(out=dst, in_=src)
             else:
@@ -123,8 +148,8 @@ def tile_sparseconv2d_kernel(tc, inputs, kernel, out):
             )
 
         regroup(0, "v", 0, H)
-        regroup(1, "v", 0, SPLIT)
-        regroup(1, "s", SPLIT, H)
+        regroup(1, "v", 0, 12)
+        regroup(1, "s", 12, H)
         quantise_image(0)
         for g0 in (0, 2, 4):
             weights_transpose(g0)
@@ -134,24 +159,22 @@ def tile_sparseconv2d_kernel(tc, inputs, kernel, out):
         weights_quantise(6)
         weights_transpose(8)
         weights_quantise(8)
-        regroup(3, "s", SPLIT, H)
-        regroup(3, "v", 0, SPLIT)
+        regroup(3, "s", 10, H)
+        regroup(3, "v", 0, 10)
         for i in range(KH):
             multiply(0, i)
-        collect(0, 0)
         quantise_image(1)
+        collect(0, 0)
         regroup(4, "s", 0, H)
         regroup(5, "v", 0, H)
-        for i in range(KH):
-            multiply(1, i)
+        multiply_shift_major(1)
         regroup(6, "s", 0, H)
         quantise_image(2)
         collect(0, 1)
         collect(0, 2)
         store(0)
+        regroup(7, "s", 0, H)
         collect(1, 0)
-        regroup(7, "v", 0, SPLIT)
-        regroup(7, "s", SPLIT, H)
         quantise_image(3)
         for i in range(KH):
             multiply(2, i)
@@ -162,9 +185,8 @@ def tile_sparseconv2d_kernel(tc, inputs, kernel, out):
         collect(2, 1)
         collect(2, 2)
         store(2)
-        for i in range(KH):
-            multiply(3, i)
-        collect(3, 0)
-        collect(3, 1)
-        collect(3, 2)
+        for d0 in (0, 8):
+            for i in range(KH):
+                multiply(3, i, d0, d0 + 8)
+                collect(3, i, d0, d0 + 8)
         store(3)

@@ -34,7 +34,7 @@ def tile_sparseconv2d_kernel(tc, inputs, kernel, out):
         raw = keep.tile([P, B, 4, H * W], BF16, name="raw")
 
         def load_image(b):
-            nc.sync.dma_start(out=raw[:, b, :, :], in_=inputs[b].rearrange("(p t) h w -> p t (h w)", t=4))
+            nc.sync.dma_start(out=raw[:, b, :, :].rearrange("p (u e) s -> p u (e s)", e=2), in_=inputs[b].rearrange("(u p e) h w -> p u (e h w)", u=2, e=2))
 
         def load_weights(g0):
             cols = slice(g0 * C, min(g0 + 2, NPASS) * C)
@@ -47,7 +47,7 @@ def tile_sparseconv2d_kernel(tc, inputs, kernel, out):
         for b in range(2, B):
             load_image(b)
 
-        kwords = kw[:].bitcast(F32).rearrange("p (g q u) -> p g u q", q=P, u=2)
+        kwords = kw[:].bitcast(F32).rearrange("p (g u q) -> p g u q", q=P, u=2)
         wgrp = keep.tile([P, NPASS * 4 * F], BF16, name="wgrp", align_bytes=64)
         wgrp_words = wgrp[:].bitcast(F32).rearrange("p (g f u) -> p g f u", f=F, u=2)
         wcodes = keep.tile([P, NPASS * F], U32, name="wcodes", align_bytes=64)
@@ -133,6 +133,12 @@ def tile_sparseconv2d_kernel(tc, inputs, kernel, out):
                         stop=(j == KW - 1),
                     )
 
+        warm = psum.tile([P, N], F32, name="warm", tag="bank")
+        first_image = raw[:, 0, :, :].rearrange("p t s -> p (t s)")
+
+        def warm_up():
+            nc.tensor.matmul(out=warm[:], lhsT=first_image[:, 0:P], rhs=first_image[:, 0:N], start=True, stop=True)
+
         def collect(g, i, d0=0, d1=OD):
             src = banks[(g, i, d0)][:].rearrange("p (d b w) -> p b w d", d=d1 - d0, b=GB)[:, :, i:i + OA, :]
             dst = osb[:, g, :].rearrange("p (b a d) -> p b a d", b=GB, a=OA)[:, :, :, d0:d1]
@@ -151,10 +157,14 @@ def tile_sparseconv2d_kernel(tc, inputs, kernel, out):
         regroup(1, "v", 0, 12)
         regroup(1, "s", 12, H)
         quantise_image(0)
+        warm_up()
+        warm_up()
         for g0 in (0, 2, 4):
             weights_transpose(g0)
+            warm_up()
             weights_quantise(g0)
         weights_transpose(6)
+        warm_up()
         regroup(2, "v", 0, H)
         weights_quantise(6)
         weights_transpose(8)

@@ -133,12 +133,6 @@ def tile_sparseconv2d_kernel(tc, inputs, kernel, out):
                         stop=(j == KW - 1),
                     )
 
-        warm = psum.tile([P, N], F32, name="warm", tag="bank")
-        first_image = raw[:, 0, :, :].rearrange("p t s -> p (t s)")
-
-        def warm_up():
-            nc.tensor.matmul(out=warm[:], lhsT=first_image[:, 0:P], rhs=first_image[:, 0:N], start=True, stop=True)
-
         def collect(g, i, d0=0, d1=OD):
             src = banks[(g, i, d0)][:].rearrange("p (d b w) -> p b w d", d=d1 - d0, b=GB)[:, :, i:i + OA, :]
             dst = osb[:, g, :].rearrange("p (b a d) -> p b a d", b=GB, a=OA)[:, :, :, d0:d1]
@@ -157,14 +151,10 @@ def tile_sparseconv2d_kernel(tc, inputs, kernel, out):
         regroup(1, "v", 0, 12)
         regroup(1, "s", 12, H)
         quantise_image(0)
-        warm_up()
-        warm_up()
         for g0 in (0, 2, 4):
             weights_transpose(g0)
-            warm_up()
             weights_quantise(g0)
         weights_transpose(6)
-        warm_up()
         regroup(2, "v", 0, H)
         weights_quantise(6)
         weights_transpose(8)

import concourse.mybir as mybir
from concourse.masks import make_identity

F32 = mybir.dt.float32
BF16 = mybir.dt.bfloat16
I32 = mybir.dt.int32
U32 = mybir.dt.uint32
U8 = mybir.dt.uint8
FP8X4 = mybir.dt.float8_e4m3fn_x4
ADD = mybir.AluOpType.add

P = 128
B, C, H, W, F = 8, 512, 18, 16, 128
KH, KW = 3, 3
OA, OD = W - KH + 1, H - KW + 1
GB = 2
NG = B // GB
ROW = GB * W
N = OD * ROW
NPASS = KH * KW

FLOPS = 2 * B * OA * OD * KH * KW * C * F


def tile_sparseconv2d_kernel(tc, inputs, kernel, out):
    nc = tc.nc
    with tc.tile_pool(name="keep", bufs=1) as keep, tc.psum_pool(name="psum", bufs=8) as psum, tc.manual_schedule():
        ident = keep.tile([P, P], F32, name="ident")
        make_identity(nc, ident[:])
        xscales = keep.tile([P, NG, H * ROW], U8, name="xscales", align_bytes=64)
        nc.vector.memset(xscales[:].rearrange("p g c -> p (g c)").bitcast(I32), 0)

        kw = keep.tile([P, NPASS * C], BF16, name="kw")
        raw = keep.tile([P, B, 4, H * W], BF16, name="raw")

        def load_image(b):
            nc.sync.dma_start(out=raw[:, b, :, :].rearrange("p (u e) s -> p u (e s)", e=2), in_=inputs[b].rearrange("(u p e) h w -> p u (e h w)", u=2, e=2))

        def load_weights(g0):
            cols = slice(g0 * C, min(g0 + 2, NPASS) * C)
            nc.sync.dma_start(out=kw[:, cols], in_=kernel[:, cols])

        load_image(0)
        load_image(1)
        for g0 in range(0, NPASS, 2):
            load_weights(g0)
        for b in range(2, B):
            load_image(b)

        kwords = kw[:].bitcast(F32).rearrange("p (g u q) -> p g u q", q=P, u=2)
        wgrp = keep.tile([P, NPASS * 4 * F], BF16, name="wgrp", align_bytes=64)
        wgrp_words = wgrp[:].bitcast(F32).rearrange("p (g f u) -> p g f u", f=F, u=2)
        wcodes = keep.tile([P, NPASS * F], U32, name="wcodes", align_bytes=64)
        wscales = keep.tile([P, NPASS * F], U8, name="wscales", align_bytes=64)
        grp = keep.tile([P, NG, H * ROW * 4], BF16, name="grp", align_bytes=64)
        xcodes = keep.tile([P, NG, H * ROW], U32, name="xcodes", align_bytes=64)
        xshift = keep.tile([P, NG, N], U8, name="xshift", align_bytes=64)
        osb = keep.tile([P, NG, GB * OA * OD], F32, name="osb")
        banks = {}

        def regroup(b, engine, h0, h1):
            dst = grp[:, b // GB, :].rearrange("p (h b w t) -> p h b w t", h=H, b=GB, w=W)[:, h0:h1, b % GB, :, :]
            src = raw[:, b, :, h0 * W:h1 * W]
            if engine == "v":
                nc.vector.tensor_copy(
                    out=dst.rearrange("p h (q i) t -> p h q t i", i=4),
                    in_=src.rearrange("p t (h q i) -> p h q t i", q=4, i=4),
                )
            else:
                nc.scalar.copy(out=dst, in_=src.rearrange("p t (h w) -> p h w t", w=W))

        def quantise_image(g):
            for h0, h1 in ((0, OD), (OD, H)):
                nc.vector.quantize_mx(
                    out=xcodes[:, g, h0 * ROW:h1 * ROW].bitcast(FP8X4),
                    scales=xscales[:, g, h0 * ROW:h1 * ROW],
                    in_=grp[:, g, h0 * ROW * 4:h1 * ROW * 4],
                )
            nc.vector.tensor_copy(out=xshift[:, g, :].bitcast(I32), in_=xscales[:, g, ROW:ROW + N].bitcast(I32))

        def weights_transpose(g0, engine="s"):
            n = min(2, NPASS - g0)
            wt = psum.tile([P, 2, 2, F], F32, name="wt", tag="bank")
            for k in range(n):
                for u in range(2):
                    nc.tensor.transpose(wt[:, k, u, :], kwords[:, g0 + k, u, :], ident[:])
            if engine == "s":
                nc.scalar.copy(out=wgrp_words[:, g0:g0 + n, :, :], in_=wt[:, 0:n, :, :].rearrange("p g u f -> p g f u"))
            else:
                nc.vector.tensor_copy(out=wgrp_words[:, g0:g0 + n, :, :], in_=wt[:, 0:n, :, :].rearrange("p g u f -> p g f u"))

        def weights_quantise(g0):
            n = min(2, NPASS - g0)
            nc.vector.quantize_mx(
                out=wcodes[:, g0 * F:(g0 + n) * F].bitcast(FP8X4),
                scales=wscales[:, g0 * F:(g0 + n) * F],
                in_=wgrp[:, g0 * 4 * F:(g0 + n) * 4 * F],
            )

        def multiply(g, i, d0=0, d1=OD):
            n = (d1 - d0) * ROW
            y = psum.tile([P, n], F32, name="y", tag="bank")
            banks[(g, i, d0)] = y
            for j in range(KW):
                k = i * KW + j
                c0 = (d0 + j) * ROW
                plane = xshift[:, g, c0 - ROW:c0 - ROW + n] if j == 1 else xscales[:, g, c0:c0 + n]
                nc.tensor.matmul_mx(
                    out=y[:],
                    lhsT=wcodes[:, k * F:(k + 1) * F].bitcast(FP8X4),
                    lhsT_scale=wscales[:, k * F:(k + 1) * F],
                    rhs=xcodes[:, g, c0:c0 + n].bitcast(FP8X4),
                    rhs_scale=plane,
                    start=(j == 0),
                    stop=(j == KW - 1),
                )

        def multiply_shift_major(g):
            ys = [psum.tile([P, N], F32, name="y%d" % i, tag="bank") for i in range(KH)]
            for j in range(KW):
                for i in range(KH):
                    banks[(g, i, 0)] = ys[i]
                    k = i * KW + j
                    c0 = j * ROW
                    plane = xshift[:, g, :] if j == 1 else xscales[:, g, c0:c0 + N]
                    nc.tensor.matmul_mx(
                        out=ys[i][:],
                        lhsT=wcodes[:, k * F:(k + 1) * F].bitcast(FP8X4),
                        lhsT_scale=wscales[:, k * F:(k + 1) * F],
                        rhs=xcodes[:, g, c0:c0 + N].bitcast(FP8X4),
                        rhs_scale=plane,
                        start=(j == 0),
                        stop=(j == KW - 1),
                    )

        def collect(g, i, d0=0, d1=OD):
            src = banks[(g, i, d0)][:].rearrange("p (d b w) -> p b w d", d=d1 - d0, b=GB)[:, :, i:i + OA, :]
            dst = osb[:, g, :].rearrange("p (b a d) -> p b a d", b=GB, a=OA)[:, :, :, d0:d1]
            if i == 0:
                nc.scalar.copy(out=dst, in_=src)
            else:
                nc.vector.tensor_tensor(out=dst, in0=src, in1=dst, op=ADD)

        def store(g):
            nc.sync.dma_start(
                out=out[g * GB:(g + 1) * GB].rearrange("b f a d -> f b (a d)"),
                in_=osb[:, g, :].rearrange("p (b s) -> p b s", b=GB),
            )

        regroup(0, "v", 0, H)
        regroup(1, "v", 0, 12)
        regroup(1, "s", 12, H)
        quantise_image(0)
        for g0 in (0, 2, 4):
            weights_transpose(g0)
            weights_quantise(g0)
        weights_transpose(6)
        regroup(2, "v", 0, H)
        weights_quantise(6)
        weights_transpose(8)
        weights_quantise(8)
        regroup(3, "s", 10, H)
        regroup(3, "v", 0, 10)
        for i in range(KH):
            multiply(0, i)
        quantise_image(1)
        collect(0, 0)
        regroup(4, "s", 0, H)
        regroup(5, "v", 0, H)
        multiply_shift_major(1)
        regroup(6, "s", 0, H)
        quantise_image(2)
        collect(0, 1)
        collect(0, 2)
        store(0)
        regroup(7, "s", 0, H)
        collect(1, 0)
        quantise_image(3)
        for i in range(KH):
            multiply(2, i)
        collect(2, 0)
        collect(1, 1)
        collect(1, 2)
        store(1)
        collect(2, 1)
        collect(2, 2)
        store(2)
        for d0 in (0, 8):
            for i in range(KH):
                multiply(3, i, d0, d0 + 8)
                collect(3, i, d0, d0 + 8)
        store(3)
